import numpy as np
import ml_dtypes


def mxq(x, axis, fmt="e4m3"):
    dtype, down = {"e4m3": (ml_dtypes.float8_e4m3fn, 7), "e5m2": (ml_dtypes.float8_e5m2, 14)}[fmt]
    v = np.moveaxis(np.asarray(x, np.float32).astype(ml_dtypes.bfloat16).astype(np.float64), axis, -1)
    blocks = v.reshape(v.shape[:-1] + (-1, 32))
    amax = np.abs(blocks).max(-1, keepdims=True)
    byte = np.maximum(np.where(amax > 0, np.frexp(amax)[1] - 1 + 127, 0) - down, 1)
    scale = np.exp2(byte - 127.0)
    codes = (blocks / scale).astype(np.float32).astype(dtype).astype(np.float64)
    return np.moveaxis((codes * scale).reshape(v.shape), -1, axis)


WIDE = False


def mx_kscale(k):
    if not WIDE:
        return np.ones(k)
    levels = np.array([10, -10, 5, -5, 0])
    a = np.random.permutation(np.resize(levels, k // 512 * 4)).reshape(k // 512, 4)
    idx = np.arange(k)
    return np.exp2(a[idx // 512, idx % 128 // 32])


BF16 = ml_dtypes.bfloat16


def bf(x):
    return np.asarray(x, np.float32).astype(BF16)


def f64(x):
    return np.asarray(x).astype(np.float64)


E2M1 = np.array([0.0, 0.5, 1.0, 1.5, 2.0, 3.0, 4.0, 6.0, -0.0, -0.5, -1.0, -1.5, -2.0, -3.0, -4.0, -6.0])


def pack_weight(w, fmt):
    k, n = w.shape
    w = f64(bf(w)).reshape(k // 32, 32, n)
    amax = np.abs(w).max(1)
    if fmt == "e4m3":
        byte = np.frexp(amax)[1] - 1 + 127 - 7
    else:
        mant, ex = np.frexp(amax / 6.0)
        byte = np.where(mant > 0.5, ex, ex - 1) + 127
    byte = np.clip(np.where(amax > 0, byte, 1), 1, 254)
    scaled = (w * np.exp2(127.0 - byte)[:, None, :]).reshape(k, n).astype(np.float32)
    by_word = np.ascontiguousarray(scaled.reshape(k // 512, 128, 4, n).transpose(0, 1, 3, 2))
    if fmt == "e4m3":
        words = by_word.astype(ml_dtypes.float8_e4m3fn).view(np.uint8)
    else:
        c = by_word.astype(ml_dtypes.float4_e2m1fn).view(np.uint8) & 0xF
        words = c[..., 0::2] | (c[..., 1::2] << 4)
    return np.ascontiguousarray(words), np.ascontiguousarray(byte.astype(np.uint8).reshape(k // 512, 16, n))


def unpack_weight(words, scales, fmt):
    g, p, n, _ = words.shape
    if fmt == "e4m3":
        vals = np.ascontiguousarray(words).view(ml_dtypes.float8_e4m3fn).astype(np.float64)
    else:
        nib = np.empty((g, p, n, 4), np.uint8)
        nib[..., 0::2] = words & 0xF
        nib[..., 1::2] = words >> 4
        vals = E2M1[nib]
    vals = vals * np.repeat(np.exp2(scales.astype(np.float64) - 127.0), 8, axis=1)[..., None]
    return vals.transpose(0, 1, 3, 2).reshape(g * 512, n)

def pack4(w):
    words, scales = pack_weight(w, "e2m1")
    return words.reshape(words.shape[0], 128, -1), scales


def unpack4(words, scales):
    return unpack_weight(words.reshape(words.shape[0], 128, -1, 2), scales, "e2m1")


B, N, D, H, DK, DV = 4, 128, 16384, 8, 64, 64


def xnorm(x, g):
    n = np.sqrt(np.sum(x * x, axis=-1, keepdims=True))
    return x * g / n


def setup_inputs():
    s = mx_kscale(D)
    queries = bf(np.random.standard_normal((B, N, D)) * s)
    Wq_words, Wq_scales = pack4(np.random.standard_normal((D, H * DK)) / np.sqrt(D) / s[:, None])
    return {
        "queries": queries,
        "Wq_words": Wq_words,
        "Wq_scales": Wq_scales,
        "bq": bf(np.random.standard_normal(H * DK) * 0.1),
        "gamma": bf(np.random.standard_normal((1, H, 1, 1)) * 2.0),
    }


def reference(queries, Wq_words, Wq_scales, bq, gamma):
    q = ((mxq(f64(queries), 2, "e4m3") @ unpack4(Wq_words, Wq_scales)) + f64(bq)).reshape(B, N, H, DK)
    return xnorm(q.transpose(0, 2, 1, 3), f64(gamma))

@@ -1,0 +1,175 @@
+from contextlib import ExitStack
+
+import concourse.mybir as mybir
+from concourse.masks import make_identity
+
+F32 = mybir.dt.float32
+BF16 = mybir.dt.bfloat16
+I32 = mybir.dt.int32
+U32 = mybir.dt.uint32
+U8 = mybir.dt.uint8
+FP8X4 = mybir.dt.float8_e4m3fn_x4
+FP4X4 = mybir.dt.float4_e2m1fn_x4
+ADD = mybir.AluOpType.add
+MULT = mybir.AluOpType.mult
+ACT = mybir.ActivationFunctionType
+
+P = 128
+BATCHES = 4
+D = 16384
+HEADS = 8
+HEAD_DIM = 64
+N_OUT = HEADS * HEAD_DIM
+K_GROUP = 512
+GROUPS = D // K_GROUP
+ROUND_GROUPS = 8
+CHUNKS = GROUPS // ROUND_GROUPS
+ROUNDS = CHUNKS * BATCHES
+K_ROUND = ROUND_GROUPS * K_GROUP
+BANK_GROUPS = 2
+ROUND_BANKS = ROUND_GROUPS // BANK_GROUPS
+RAW_BUFS = 6
+
+FLOPS = 2 * BATCHES * P * D * N_OUT
+
+
+def tile_ufoattention_pb_k_kernel(tc, queries, Wq_words, Wq_scales, bq, gamma, out):
+    nc = tc.nc
+    with ExitStack() as ctx:
+        ctx.enter_context(tc.manual_schedule())
+        keep = ctx.enter_context(tc.tile_pool(name="keep", bufs=1))
+        raw_pool = ctx.enter_context(tc.tile_pool(name="raw", bufs=RAW_BUFS))
+        sort_pool = ctx.enter_context(tc.tile_pool(name="sort", bufs=3))
+        group_pool = ctx.enter_context(tc.tile_pool(name="group", bufs=2))
+        code_pool = ctx.enter_context(tc.tile_pool(name="code", bufs=3))
+        end_pool = ctx.enter_context(tc.tile_pool(name="end", bufs=2))
+        sum_psum = ctx.enter_context(tc.psum_pool(name="sums", bufs=1))
+        flip_psum = ctx.enter_context(tc.psum_pool(name="flip", bufs=ROUND_BANKS))
+
+        w_words = keep.tile([P, GROUPS, 2 * N_OUT], U8, align_bytes=64)
+        w_planes = keep.tile([P, GROUPS, N_OUT], U8, align_bytes=64)
+        ident = keep.tile([P, P], F32)
+        bias = keep.tile([P, HEADS, HEAD_DIM], BF16)
+        gains = keep.tile([P, HEADS], BF16)
+        one = keep.tile([P, 1], F32)
+        one_root = keep.tile([P, 1], F32)
+        sums = [sum_psum.tile([P, N_OUT], F32, name="sums%d" % b) for b in range(BATCHES)]
+
+        words_dram = Wq_words.bitcast(I32)
+        scales_dram = Wq_scales.bitcast(I32).rearrange("g (j q) n -> q j g n", j=2)
+
+        for c in range(CHUNKS):
+            chunk = slice(c * ROUND_GROUPS, (c + 1) * ROUND_GROUPS)
+            nc.vector.memset(w_planes[:, chunk, :].bitcast(I32), 0)
+        make_identity(nc, ident[:])
+        nc.vector.memset(one[:], 1.0)
+        nc.scalar.activation(out=one_root[:], in_=one[:], func=ACT.Sqrt)
+
+        raw = {}
+        sorted_words = {}
+        codes = {}
+        planes = {}
+
+        def load_weights(c):
+            chunk = slice(c * ROUND_GROUPS, (c + 1) * ROUND_GROUPS)
+            for q in range(8):
+                first = 32 * (q // 4) + q % 4
+                nc.sync.dma_start(
+                    out=w_planes[first:P:64, chunk, :].bitcast(I32), in_=scales_dram[q, :, chunk, :]
+                )
+            nc.sync.dma_start(
+                out=w_words[:, chunk, :].bitcast(I32), in_=words_dram[chunk].rearrange("g p n -> p g n")
+            )
+
+        def load_round(r):
+            c, b = divmod(r, BATCHES)
+            raw[r] = raw_pool.tile([P, K_ROUND], BF16, name="raw")
+            nc.sync.dma_start(out=raw[r][:], in_=queries[b, :, c * K_ROUND : (c + 1) * K_ROUND])
+            if b == 1:
+                load_weights(c)
+
+        def sort_round(r):
+            sorted_words[r] = sort_pool.tile([P, ROUND_GROUPS, 2, P], F32, name="sorted_words")
+            nc.vector.tensor_copy(
+                out=sorted_words[r][:],
+                in_=raw[r][:].bitcast(F32).rearrange("m (g p u) -> m g u p", g=ROUND_GROUPS, u=2),
+            )
+
+        def transpose_round(r):
+            grouped = group_pool.tile([P, ROUND_GROUPS, P, 2], F32, name="grouped", align_bytes=64)
+            source = sorted_words[r]
+            for bank in range(ROUND_BANKS):
+                flipped = flip_psum.tile([P, BANK_GROUPS, 2, P], F32, name="flipped")
+                for j in range(BANK_GROUPS):
+                    for u in range(2):
+                        nc.tensor.transpose(flipped[:, j, u, :], source[:, bank * BANK_GROUPS + j, u, :], ident[:])
+                nc.scalar.copy(
+                    out=grouped[:, bank * BANK_GROUPS : (bank + 1) * BANK_GROUPS, :, :],
+                    in_=flipped[:].rearrange("p j u m -> p j m u"),
+                )
+            return grouped
+
+        def quantise_round(r, grouped):
+            codes[r] = code_pool.tile([P, ROUND_GROUPS * P], U32, name="codes", align_bytes=64)
+            planes[r] = code_pool.tile([P, ROUND_GROUPS * P], U8, name="planes", align_bytes=64)
+            values = grouped[:].rearrange("p g m u -> p (g m u)").bitcast(BF16)
+            half = ROUND_GROUPS * P // 2
+            for h in range(2):
+                nc.vector.quantize_mx(
+                    out=codes[r][:, h * half : (h + 1) * half].bitcast(FP8X4),
+                    scales=planes[r][:, h * half : (h + 1) * half],
+                    in_=values[:, 4 * h * half : 4 * (h + 1) * half],
+                )
+
+        def multiply_round(r):
+            c, b = divmod(r, BATCHES)
+            round_codes = codes[r]
+            round_planes = planes[r]
+            for j in range(ROUND_GROUPS):
+                g = c * ROUND_GROUPS + j
+                nc.tensor.matmul_mx(
+                    out=sums[b][:],
+                    lhsT=round_codes[:, j * P : (j + 1) * P].bitcast(FP8X4),
+                    lhsT_scale=round_planes[:, j * P : (j + 1) * P],
+                    rhs=w_words[:, g, :].bitcast(FP4X4),
+                    rhs_scale=w_planes[:, g, :],
+                    start=(g == 0),
+                    stop=(g == GROUPS - 1),
+                )
+
+        def finish_batch(b):
+            q_sb = end_pool.tile([P, HEADS, HEAD_DIM], F32, name="q_sb")
+            nc.vector.tensor_tensor(
+                out=q_sb[:], in0=sums[b][:].rearrange("p (h d) -> p h d", h=HEADS), in1=bias[:], op=ADD
+            )
+            squares = end_pool.tile([P, HEADS, HEAD_DIM], F32, name="squares")
+            nc.scalar.activation(out=squares[:], in_=q_sb[:], func=ACT.Square)
+            norm2 = end_pool.tile([P, HEADS], F32, name="norm2")
+            nc.vector.tensor_reduce(out=norm2[:], in_=squares[:], axis=mybir.AxisListType.X, op=ADD)
+            norm = end_pool.tile([P, HEADS], F32, name="norm")
+            nc.scalar.activation(out=norm[:], in_=norm2[:], func=ACT.Sqrt)
+            factor = end_pool.tile([P, HEADS], F32, name="factor")
+            nc.vector.reciprocal(out=factor[:], in_=norm[:])
+            nc.vector.tensor_tensor(out=factor[:], in0=factor[:], in1=gains[:], op=MULT)
+            result = end_pool.tile([P, HEADS, HEAD_DIM], F32, name="result")
+            nc.vector.tensor_tensor(
+                out=result[:], in0=q_sb[:], in1=factor[:].unsqueeze(2).to_broadcast([P, HEADS, HEAD_DIM]), op=MULT
+            )
+            nc.sync.dma_start(out=out[b].rearrange("h n d -> n h d"), in_=result[:])
+
+        for r in range(RAW_BUFS):
+            load_round(r)
+        nc.sync.dma_start(out=bias[:].rearrange("p h d -> p (h d)"), in_=bq.partition_broadcast(P))
+        nc.sync.dma_start(out=gains[:], in_=gamma.rearrange("a h b c -> (a h b c)").partition_broadcast(P))
+
+        for i in range(-2, ROUNDS + 1):
+            if i + 2 < ROUNDS:
+                sort_round(i + 2)
+                if i + 2 + RAW_BUFS < ROUNDS:
+                    load_round(i + 2 + RAW_BUFS)
+            if 0 <= i + 1 < ROUNDS:
+                quantise_round(i + 1, transpose_round(i + 1))
+            if 0 <= i < ROUNDS:
+                multiply_round(i)
+            if i - 1 >= ROUNDS - BATCHES:
+                finish_batch(i - 1 - (ROUNDS - BATCHES))

@@ -25,6 +25,7 @@ GROUPS = D // K_GROUP
 ROUND_GROUPS = 8
 CHUNKS = GROUPS // ROUND_GROUPS
 ROUNDS = CHUNKS * BATCHES
+ORDER = [(c, b) for c in range(CHUNKS) for b in range(BATCHES)]
 K_ROUND = ROUND_GROUPS * K_GROUP
 BANK_GROUPS = 2
 ROUND_BANKS = ROUND_GROUPS // BANK_GROUPS
@@ -46,8 +47,8 @@ def tile_ufoattention_pb_k_kernel(tc, queries, Wq_words, Wq_scales, bq, gamma, o
         sum_psum = ctx.enter_context(tc.psum_pool(name="sums", bufs=1))
         flip_psum = ctx.enter_context(tc.psum_pool(name="flip", bufs=ROUND_BANKS))
 
-        w_words = keep.tile([P, GROUPS, 2 * N_OUT], U8, align_bytes=64)
-        w_planes = keep.tile([P, GROUPS, N_OUT], U8, align_bytes=64)
+        w_words = [keep.tile([P, ROUND_GROUPS, 2 * N_OUT], U8, name="w_words%d" % c, align_bytes=64) for c in range(CHUNKS)]
+        w_planes = [keep.tile([P, ROUND_GROUPS, N_OUT], U8, name="w_planes%d" % c, align_bytes=64) for c in range(CHUNKS)]
         ident = keep.tile([P, P], F32)
         bias = keep.tile([P, HEADS, HEAD_DIM], BF16)
         gains = keep.tile([P, HEADS], BF16)
@@ -59,8 +60,7 @@ def tile_ufoattention_pb_k_kernel(tc, queries, Wq_words, Wq_scales, bq, gamma, o
         scales_dram = Wq_scales.bitcast(I32).rearrange("g (j q) n -> q j g n", j=2)
 
         for c in range(CHUNKS):
-            chunk = slice(c * ROUND_GROUPS, (c + 1) * ROUND_GROUPS)
-            nc.vector.memset(w_planes[:, chunk, :].bitcast(I32), 0)
+            nc.vector.memset(w_planes[c][:].bitcast(I32), 0)
         make_identity(nc, ident[:])
         nc.vector.memset(one[:], 1.0)
         nc.scalar.activation(out=one_root[:], in_=one[:], func=ACT.Sqrt)
@@ -75,14 +75,14 @@ def tile_ufoattention_pb_k_kernel(tc, queries, Wq_words, Wq_scales, bq, gamma, o
             for q in range(8):
                 first = 32 * (q // 4) + q % 4
                 nc.sync.dma_start(
-                    out=w_planes[first:P:64, chunk, :].bitcast(I32), in_=scales_dram[q, :, chunk, :]
+                    out=w_planes[c][first:P:64, :, :].bitcast(I32), in_=scales_dram[q, :, chunk, :]
                 )
             nc.sync.dma_start(
-                out=w_words[:, chunk, :].bitcast(I32), in_=words_dram[chunk].rearrange("g p n -> p g n")
+                out=w_words[c][:].bitcast(I32), in_=words_dram[chunk].rearrange("g p n -> p g n")
             )
 
         def load_round(r):
-            c, b = divmod(r, BATCHES)
+            c, b = ORDER[r]
             raw[r] = raw_pool.tile([P, K_ROUND], BF16, name="raw")
             nc.sync.dma_start(out=raw[r][:], in_=queries[b, :, c * K_ROUND : (c + 1) * K_ROUND])
             if b == 1:
@@ -122,7 +122,7 @@ def tile_ufoattention_pb_k_kernel(tc, queries, Wq_words, Wq_scales, bq, gamma, o
                 )
 
         def multiply_round(r):
-            c, b = divmod(r, BATCHES)
+            c, b = ORDER[r]
             round_codes = codes[r]
             round_planes = planes[r]
             for j in range(ROUND_GROUPS):
@@ -131,29 +131,40 @@ def tile_ufoattention_pb_k_kernel(tc, queries, Wq_words, Wq_scales, bq, gamma, o
                     out=sums[b][:],
                     lhsT=round_codes[:, j * P : (j + 1) * P].bitcast(FP8X4),
                     lhsT_scale=round_planes[:, j * P : (j + 1) * P],
-                    rhs=w_words[:, g, :].bitcast(FP4X4),
-                    rhs_scale=w_planes[:, g, :],
+                    rhs=w_words[c][:, j, :].bitcast(FP4X4),
+                    rhs_scale=w_planes[c][:, j, :],
                     start=(g == 0),
                     stop=(g == GROUPS - 1),
                 )
 
-        def finish_batch(b):
-            q_sb = end_pool.tile([P, HEADS, HEAD_DIM], F32, name="q_sb")
+        q_sb = {}
+        squares = {}
+        norm2 = {}
+
+        def add_bias(b):
+            q_sb[b] = end_pool.tile([P, HEADS, HEAD_DIM], F32, name="q_sb")
             nc.vector.tensor_tensor(
-                out=q_sb[:], in0=sums[b][:].rearrange("p (h d) -> p h d", h=HEADS), in1=bias[:], op=ADD
+                out=q_sb[b][:], in0=sums[b][:].rearrange("p (h d) -> p h d", h=HEADS), in1=bias[:], op=ADD
             )
-            squares = end_pool.tile([P, HEADS, HEAD_DIM], F32, name="squares")
-            nc.scalar.activation(out=squares[:], in_=q_sb[:], func=ACT.Square)
-            norm2 = end_pool.tile([P, HEADS], F32, name="norm2")
-            nc.vector.tensor_reduce(out=norm2[:], in_=squares[:], axis=mybir.AxisListType.X, op=ADD)
+
+        def square(b):
+            squares[b] = end_pool.tile([P, HEADS, HEAD_DIM], F32, name="squares")
+            nc.scalar.activation(out=squares[b][:], in_=q_sb[b][:], func=ACT.Square)
+
+        def sum_squares(b):
+            norm2[b] = end_pool.tile([P, HEADS], F32, name="norm2")
+            nc.vector.tensor_reduce(out=norm2[b][:], in_=squares[b][:], axis=mybir.AxisListType.X, op=ADD)
+
+        def scale_and_store(b):
             norm = end_pool.tile([P, HEADS], F32, name="norm")
-            nc.scalar.activation(out=norm[:], in_=norm2[:], func=ACT.Sqrt)
+            nc.scalar.activation(out=norm[:], in_=norm2[b][:], func=ACT.Sqrt)
+            inverse = end_pool.tile([P, HEADS], F32, name="inverse")
+            nc.vector.reciprocal(out=inverse[:], in_=norm[:])
             factor = end_pool.tile([P, HEADS], F32, name="factor")
-            nc.vector.reciprocal(out=factor[:], in_=norm[:])
-            nc.vector.tensor_tensor(out=factor[:], in0=factor[:], in1=gains[:], op=MULT)
+            nc.vector.tensor_tensor(out=factor[:], in0=inverse[:], in1=gains[:], op=MULT)
             result = end_pool.tile([P, HEADS, HEAD_DIM], F32, name="result")
             nc.vector.tensor_tensor(
-                out=result[:], in0=q_sb[:], in1=factor[:].unsqueeze(2).to_broadcast([P, HEADS, HEAD_DIM]), op=MULT
+                out=result[:], in0=q_sb[b][:], in1=factor[:].unsqueeze(2).to_broadcast([P, HEADS, HEAD_DIM]), op=MULT
             )
             nc.sync.dma_start(out=out[b].rearrange("h n d -> n h d"), in_=result[:])
 
@@ -163,13 +174,22 @@ def tile_ufoattention_pb_k_kernel(tc, queries, Wq_words, Wq_scales, bq, gamma, o
         nc.sync.dma_start(out=gains[:], in_=gamma.rearrange("a h b c -> (a h b c)").partition_broadcast(P))
 
         for i in range(-2, ROUNDS + 1):
+            ended = [ORDER[i - 1][1]] if i >= 1 and ORDER[i - 1][0] == CHUNKS - 1 else []
+            for b in ended:
+                add_bias(b)
             if i + 2 < ROUNDS:
                 sort_round(i + 2)
                 if i + 2 + RAW_BUFS < ROUNDS:
                     load_round(i + 2 + RAW_BUFS)
+            for b in ended:
+                square(b)
             if 0 <= i + 1 < ROUNDS:
-                quantise_round(i + 1, transpose_round(i + 1))
+                grouped = transpose_round(i + 1)
+            for b in ended:
+                sum_squares(b)
+            if 0 <= i + 1 < ROUNDS:
+                quantise_round(i + 1, grouped)
+            for b in ended:
+                scale_and_store(b)
             if 0 <= i < ROUNDS:
                 multiply_round(i)
-            if i - 1 >= ROUNDS - BATCHES:
-                finish_batch(i - 1 - (ROUNDS - BATCHES))

@@ -29,7 +29,7 @@ ORDER = [(c, b) for c in range(CHUNKS) for b in range(BATCHES)]
 K_ROUND = ROUND_GROUPS * K_GROUP
 BANK_GROUPS = 2
 ROUND_BANKS = ROUND_GROUPS // BANK_GROUPS
-RAW_BUFS = 6
+RAW_BUFS = 8
 
 FLOPS = 2 * BATCHES * P * D * N_OUT
 
@@ -57,7 +57,7 @@ def tile_ufoattention_pb_k_kernel(tc, queries, Wq_words, Wq_scales, bq, gamma, o
         sums = [sum_psum.tile([P, N_OUT], F32, name="sums%d" % b) for b in range(BATCHES)]
 
         words_dram = Wq_words.bitcast(I32)
-        scales_dram = Wq_scales.bitcast(I32).rearrange("g (j q) n -> q j g n", j=2)
+        scales_dram = Wq_scales.bitcast(I32).rearrange("g (Q r) n -> r Q g n", r=4)
 
         for c in range(CHUNKS):
             nc.vector.memset(w_planes[c][:].bitcast(I32), 0)
@@ -72,11 +72,8 @@ def tile_ufoattention_pb_k_kernel(tc, queries, Wq_words, Wq_scales, bq, gamma, o
 
         def load_weights(c):
             chunk = slice(c * ROUND_GROUPS, (c + 1) * ROUND_GROUPS)
-            for q in range(8):
-                first = 32 * (q // 4) + q % 4
-                nc.sync.dma_start(
-                    out=w_planes[c][first:P:64, :, :].bitcast(I32), in_=scales_dram[q, :, chunk, :]
-                )
+            for r in range(4):
+                nc.sync.dma_start(out=w_planes[c][r:P:32, :, :].bitcast(I32), in_=scales_dram[r, :, chunk, :])
             nc.sync.dma_start(
                 out=w_words[c][:].bitcast(I32), in_=words_dram[chunk].rearrange("g p n -> p g n")
             )
@@ -170,8 +167,6 @@ def tile_ufoattention_pb_k_kernel(tc, queries, Wq_words, Wq_scales, bq, gamma, o
 
         for r in range(RAW_BUFS):
             load_round(r)
-        nc.sync.dma_start(out=bias[:].rearrange("p h d -> p (h d)"), in_=bq.partition_broadcast(P))
-        nc.sync.dma_start(out=gains[:], in_=gamma.rearrange("a h b c -> (a h b c)").partition_broadcast(P))
 
         for i in range(-2, ROUNDS + 1):
             ended = [ORDER[i - 1][1]] if i >= 1 and ORDER[i - 1][0] == CHUNKS - 1 else []
@@ -181,6 +176,11 @@ def tile_ufoattention_pb_k_kernel(tc, queries, Wq_words, Wq_scales, bq, gamma, o
                 sort_round(i + 2)
                 if i + 2 + RAW_BUFS < ROUNDS:
                     load_round(i + 2 + RAW_BUFS)
+                if i + 2 + RAW_BUFS == ROUNDS:
+                    nc.sync.dma_start(out=bias[:].rearrange("p h d -> p (h d)"), in_=bq.partition_broadcast(P))
+                    nc.sync.dma_start(
+                        out=gains[:], in_=gamma.rearrange("a h b c -> (a h b c)").partition_broadcast(P)
+                    )
             for b in ended:
                 square(b)
             if 0 <= i + 1 < ROUNDS:

@@ -25,7 +25,9 @@ GROUPS = D // K_GROUP
 ROUND_GROUPS = 8
 CHUNKS = GROUPS // ROUND_GROUPS
 ROUNDS = CHUNKS * BATCHES
-ORDER = [(c, b) for c in range(CHUNKS) for b in range(BATCHES)]
+LAST = BATCHES - 1
+KEPT_BACK = [(c, LAST) for c in range(CHUNKS - 2, CHUNKS)]
+ORDER = [(c, b) for c in range(CHUNKS) for b in range(BATCHES) if (c, b) not in KEPT_BACK] + KEPT_BACK
 K_ROUND = ROUND_GROUPS * K_GROUP
 BANK_GROUPS = 2
 ROUND_BANKS = ROUND_GROUPS // BANK_GROUPS
@@ -181,15 +183,11 @@ def tile_ufoattention_pb_k_kernel(tc, queries, Wq_words, Wq_scales, bq, gamma, o
                     nc.sync.dma_start(
                         out=gains[:], in_=gamma.rearrange("a h b c -> (a h b c)").partition_broadcast(P)
                     )
+            if 0 <= i + 1 < ROUNDS:
+                quantise_round(i + 1, transpose_round(i + 1))
             for b in ended:
                 square(b)
-            if 0 <= i + 1 < ROUNDS:
-                grouped = transpose_round(i + 1)
-            for b in ended:
                 sum_squares(b)
-            if 0 <= i + 1 < ROUNDS:
-                quantise_round(i + 1, grouped)
-            for b in ended:
                 scale_and_store(b)
             if 0 <= i < ROUNDS:
                 multiply_round(i)

@@ -49,8 +49,8 @@ def tile_ufoattention_pb_k_kernel(tc, queries, Wq_words, Wq_scales, bq, gamma, o
         sum_psum = ctx.enter_context(tc.psum_pool(name="sums", bufs=1))
         flip_psum = ctx.enter_context(tc.psum_pool(name="flip", bufs=ROUND_BANKS))
 
-        w_words = [keep.tile([P, ROUND_GROUPS, 2 * N_OUT], U8, name="w_words%d" % c, align_bytes=64) for c in range(CHUNKS)]
-        w_planes = [keep.tile([P, ROUND_GROUPS, N_OUT], U8, name="w_planes%d" % c, align_bytes=64) for c in range(CHUNKS)]
+        w_words = [keep.tile([P, ROUND_GROUPS, 2 * N_OUT], U8, name="w_words%d" % c, align_bytes=256) for c in range(CHUNKS)]
+        w_planes = [keep.tile([P, ROUND_GROUPS, N_OUT], U8, name="w_planes%d" % c, align_bytes=256) for c in range(CHUNKS)]
         ident = keep.tile([P, P], F32)
         bias = keep.tile([P, HEADS, HEAD_DIM], BF16)
         gains = keep.tile([P, HEADS], BF16)
@@ -95,7 +95,7 @@ def tile_ufoattention_pb_k_kernel(tc, queries, Wq_words, Wq_scales, bq, gamma, o
             )
 
         def transpose_round(r):
-            grouped = group_pool.tile([P, ROUND_GROUPS, P, 2], F32, name="grouped", align_bytes=64)
+            grouped = group_pool.tile([P, ROUND_GROUPS, P, 2], F32, name="grouped", align_bytes=256)
             source = sorted_words[r]
             for bank in range(ROUND_BANKS):
                 flipped = flip_psum.tile([P, BANK_GROUPS, 2, P], F32, name="flipped")
@@ -109,8 +109,8 @@ def tile_ufoattention_pb_k_kernel(tc, queries, Wq_words, Wq_scales, bq, gamma, o
             return grouped
 
         def quantise_round(r, grouped):
-            codes[r] = code_pool.tile([P, ROUND_GROUPS * P], U32, name="codes", align_bytes=64)
-            planes[r] = code_pool.tile([P, ROUND_GROUPS * P], U8, name="planes", align_bytes=64)
+            codes[r] = code_pool.tile([P, ROUND_GROUPS * P], U32, name="codes", align_bytes=256)
+            planes[r] = code_pool.tile([P, ROUND_GROUPS * P], U8, name="planes", align_bytes=256)
             values = grouped[:].rearrange("p g m u -> p (g m u)").bitcast(BF16)
             half = ROUND_GROUPS * P // 2
             for h in range(2):
@@ -140,11 +140,16 @@ def tile_ufoattention_pb_k_kernel(tc, queries, Wq_words, Wq_scales, bq, gamma, o
         squares = {}
         norm2 = {}
 
-        def add_bias(b):
-            q_sb[b] = end_pool.tile([P, HEADS, HEAD_DIM], F32, name="q_sb")
+        def add_bias(b, h0=0, h1=HEADS):
+            if h0 == 0:
+                q_sb[b] = end_pool.tile([P, HEADS, HEAD_DIM], F32, name="q_sb")
             nc.vector.tensor_tensor(
-                out=q_sb[b][:], in0=sums[b][:].rearrange("p (h d) -> p h d", h=HEADS), in1=bias[:], op=ADD
+                out=q_sb[b][:, h0:h1, :],
+                in0=sums[b][:].rearrange("p (h d) -> p h d", h=HEADS)[:, h0:h1, :],
+                in1=bias[:, h0:h1, :],
+                op=ADD,
             )
+
 
         def square(b):
             squares[b] = end_pool.tile([P, HEADS, HEAD_DIM], F32, name="squares")
@@ -167,11 +172,45 @@ def tile_ufoattention_pb_k_kernel(tc, queries, Wq_words, Wq_scales, bq, gamma, o
             )
             nc.sync.dma_start(out=out[b].rearrange("h n d -> n h d"), in_=result[:])
 
+        def end_last_batch():
+            b = LAST
+            half = HEADS // 2
+            halves = [(0, half), (half, HEADS)]
+            for h0, h1 in halves:
+                add_bias(b, h0, h1)
+            scaled = end_pool.tile([P, HEADS, HEAD_DIM], F32, name="squares")
+            norm_sum = end_pool.tile([P, HEADS], F32, name="norm2")
+            norm = end_pool.tile([P, HEADS], F32, name="norm")
+            inverse = end_pool.tile([P, HEADS], F32, name="inverse")
+            result = end_pool.tile([P, HEADS, HEAD_DIM], F32, name="result")
+            waste = end_pool.tile([P, HEADS, HEAD_DIM], F32, name="waste")
+            for h0, h1 in halves:
+                for h in range(h0, h1):
+                    nc.scalar.activation(
+                        out=waste[:, h, :], in_=q_sb[b][:, h, :], func=ACT.Square, accum_out=norm_sum[:, h : h + 1]
+                    )
+                nc.scalar.activation(out=norm[:, h0:h1], in_=norm_sum[:, h0:h1], func=ACT.Sqrt)
+                nc.vector.tensor_tensor(
+                    out=scaled[:, h0:h1, :],
+                    in0=q_sb[b][:, h0:h1, :],
+                    in1=gains[:, h0:h1].unsqueeze(2).to_broadcast([P, h1 - h0, HEAD_DIM]),
+                    op=MULT,
+                )
+            for h0, h1 in halves:
+                nc.vector.reciprocal(out=inverse[:, h0:h1], in_=norm[:, h0:h1])
+                nc.vector.tensor_tensor(
+                    out=result[:, h0:h1, :],
+                    in0=scaled[:, h0:h1, :],
+                    in1=inverse[:, h0:h1].unsqueeze(2).to_broadcast([P, h1 - h0, HEAD_DIM]),
+                    op=MULT,
+                )
+                nc.sync.dma_start(out=out[b, h0:h1].rearrange("h n d -> n h d"), in_=result[:, h0:h1, :])
+
         for r in range(RAW_BUFS):
             load_round(r)
 
-        for i in range(-2, ROUNDS + 1):
-            ended = [ORDER[i - 1][1]] if i >= 1 and ORDER[i - 1][0] == CHUNKS - 1 else []
+        for i in range(-2, ROUNDS):
+            ended = [ORDER[i - 1][1]] if i >= 1 and ORDER[i - 1][0] == CHUNKS - 1 and ORDER[i - 1][1] != LAST else []
             for b in ended:
                 add_bias(b)
             if i + 2 < ROUNDS:
@@ -191,3 +230,4 @@ def tile_ufoattention_pb_k_kernel(tc, queries, Wq_words, Wq_scales, bq, gamma, o
                 scale_and_store(b)
             if 0 <= i < ROUNDS:
                 multiply_round(i)
+        end_last_batch()

@@ -22,16 +22,19 @@ HEAD_DIM = 64
 N_OUT = HEADS * HEAD_DIM
 K_GROUP = 512
 GROUPS = D // K_GROUP
-ROUND_GROUPS = 8
-CHUNKS = GROUPS // ROUND_GROUPS
-ROUNDS = CHUNKS * BATCHES
+CHUNK_GROUPS = [4, 4, 8, 8, 8]
+CHUNKS = len(CHUNK_GROUPS)
+CHUNK_START = [sum(CHUNK_GROUPS[:c]) for c in range(CHUNKS)]
 LAST = BATCHES - 1
 KEPT_BACK = [(c, LAST) for c in range(CHUNKS - 2, CHUNKS)]
-ORDER = [(c, b) for c in range(CHUNKS) for b in range(BATCHES) if (c, b) not in KEPT_BACK] + KEPT_BACK
-K_ROUND = ROUND_GROUPS * K_GROUP
+PIECES = [(c, b) for c in range(CHUNKS) for b in range(BATCHES) if (c, b) not in KEPT_BACK] + KEPT_BACK
+RUN_PIECES = [1] * 4 + [2] * 2 + [1] * 12
+DEEPER = 8
 BANK_GROUPS = 2
-ROUND_BANKS = ROUND_GROUPS // BANK_GROUPS
-RAW_BUFS = 8
+FLIP_BANKS = 4
+MAX_GROUPS = max(CHUNK_GROUPS)
+RAW_BUFS = 7
+QUANT_GROUPS = 4
 
 FLOPS = 2 * BATCHES * P * D * N_OUT
 
@@ -42,15 +45,15 @@ def tile_ufoattention_pb_k_kernel(tc, queries, Wq_words, Wq_scales, bq, gamma, o
         ctx.enter_context(tc.manual_schedule())
         keep = ctx.enter_context(tc.tile_pool(name="keep", bufs=1))
         raw_pool = ctx.enter_context(tc.tile_pool(name="raw", bufs=RAW_BUFS))
-        sort_pool = ctx.enter_context(tc.tile_pool(name="sort", bufs=3))
+        sort_pool = ctx.enter_context(tc.tile_pool(name="sort", bufs=4))
         group_pool = ctx.enter_context(tc.tile_pool(name="group", bufs=2))
-        code_pool = ctx.enter_context(tc.tile_pool(name="code", bufs=3))
+        code_pool = ctx.enter_context(tc.tile_pool(name="code", bufs=4))
         end_pool = ctx.enter_context(tc.tile_pool(name="end", bufs=2))
         sum_psum = ctx.enter_context(tc.psum_pool(name="sums", bufs=1))
-        flip_psum = ctx.enter_context(tc.psum_pool(name="flip", bufs=ROUND_BANKS))
+        flip_psum = ctx.enter_context(tc.psum_pool(name="flip", bufs=FLIP_BANKS))
 
-        w_words = [keep.tile([P, ROUND_GROUPS, 2 * N_OUT], U8, name="w_words%d" % c, align_bytes=256) for c in range(CHUNKS)]
-        w_planes = [keep.tile([P, ROUND_GROUPS, N_OUT], U8, name="w_planes%d" % c, align_bytes=256) for c in range(CHUNKS)]
+        w_words = [keep.tile([P, g, 2 * N_OUT], U8, name="w_words%d" % c, align_bytes=256) for c, g in enumerate(CHUNK_GROUPS)]
+        w_planes = [keep.tile([P, g, N_OUT], U8, name="w_planes%d" % c, align_bytes=256) for c, g in enumerate(CHUNK_GROUPS)]
         ident = keep.tile([P, P], F32)
         bias = keep.tile([P, HEADS, HEAD_DIM], BF16)
         gains = keep.tile([P, HEADS], BF16)
@@ -61,75 +64,91 @@ def tile_ufoattention_pb_k_kernel(tc, queries, Wq_words, Wq_scales, bq, gamma, o
         words_dram = Wq_words.bitcast(I32)
         scales_dram = Wq_scales.bitcast(I32).rearrange("g (Q r) n -> r Q g n", r=4)
 
-        for c in range(CHUNKS):
-            nc.vector.memset(w_planes[c][:].bitcast(I32), 0)
-        make_identity(nc, ident[:])
         nc.vector.memset(one[:], 1.0)
+
+        def clear_planes(c):
+            nc.vector.memset(w_planes[c][:].bitcast(I32), 0)
+
+        for c in range(2):
+            clear_planes(c)
+        make_identity(nc, ident[:])
         nc.scalar.activation(out=one_root[:], in_=one[:], func=ACT.Sqrt)
 
         raw = {}
         sorted_words = {}
+        grouped = {}
         codes = {}
         planes = {}
 
         def load_weights(c):
-            chunk = slice(c * ROUND_GROUPS, (c + 1) * ROUND_GROUPS)
+            chunk = slice(CHUNK_START[c], CHUNK_START[c] + CHUNK_GROUPS[c])
             for r in range(4):
                 nc.sync.dma_start(out=w_planes[c][r:P:32, :, :].bitcast(I32), in_=scales_dram[r, :, chunk, :])
             nc.sync.dma_start(
                 out=w_words[c][:].bitcast(I32), in_=words_dram[chunk].rearrange("g p n -> p g n")
             )
 
-        def load_round(r):
-            c, b = ORDER[r]
-            raw[r] = raw_pool.tile([P, K_ROUND], BF16, name="raw")
-            nc.sync.dma_start(out=raw[r][:], in_=queries[b, :, c * K_ROUND : (c + 1) * K_ROUND])
+        def load_piece(r):
+            c, b = PIECES[r]
+            n = CHUNK_GROUPS[c]
+            if n == MAX_GROUPS:
+                raw[r] = raw_pool.tile([P, n * K_GROUP], BF16, name="raw")
+            else:
+                raw[r] = keep.tile([P, n * K_GROUP], BF16, name="raw_%d_%d" % (c, b))
+            k0 = CHUNK_START[c] * K_GROUP
+            part = n * K_GROUP // (2 if r == 0 else 1)
+            for start in range(0, n * K_GROUP, part):
+                nc.sync.dma_start(
+                    out=raw[r][:, start : start + part], in_=queries[b, :, k0 + start : k0 + start + part]
+                )
             if b == 1:
                 load_weights(c)
 
-        def sort_round(r):
-            sorted_words[r] = sort_pool.tile([P, ROUND_GROUPS, 2, P], F32, name="sorted_words")
-            nc.vector.tensor_copy(
-                out=sorted_words[r][:],
-                in_=raw[r][:].bitcast(F32).rearrange("m (g p u) -> m g u p", g=ROUND_GROUPS, u=2),
-            )
+        def sort_piece(r):
+            n = CHUNK_GROUPS[PIECES[r][0]]
+            sorted_words[r] = sort_pool.tile([P, n, 2, P], F32, name="sorted_words")
+            words = raw[r][:].bitcast(F32).rearrange("m (g p u) -> m g u p", g=n, u=2)
+            part = n // (2 if r == 0 else 1)
+            for start in range(0, n, part):
+                nc.vector.tensor_copy(
+                    out=sorted_words[r][:, start : start + part, :, :], in_=words[:, start : start + part, :, :]
+                )
 
-        def transpose_round(r):
-            grouped = group_pool.tile([P, ROUND_GROUPS, P, 2], F32, name="grouped", align_bytes=256)
+        def flip_piece(r):
+            n = CHUNK_GROUPS[PIECES[r][0]]
+            grouped[r] = group_pool.tile([P, n, P, 2], F32, name="grouped", align_bytes=256)
             source = sorted_words[r]
-            for bank in range(ROUND_BANKS):
+            for bank in range(n // BANK_GROUPS):
                 flipped = flip_psum.tile([P, BANK_GROUPS, 2, P], F32, name="flipped")
                 for j in range(BANK_GROUPS):
                     for u in range(2):
                         nc.tensor.transpose(flipped[:, j, u, :], source[:, bank * BANK_GROUPS + j, u, :], ident[:])
                 nc.scalar.copy(
-                    out=grouped[:, bank * BANK_GROUPS : (bank + 1) * BANK_GROUPS, :, :],
+                    out=grouped[r][:, bank * BANK_GROUPS : (bank + 1) * BANK_GROUPS, :, :],
                     in_=flipped[:].rearrange("p j u m -> p j m u"),
                 )
-            return grouped
 
-        def quantise_round(r, grouped):
-            codes[r] = code_pool.tile([P, ROUND_GROUPS * P], U32, name="codes", align_bytes=256)
-            planes[r] = code_pool.tile([P, ROUND_GROUPS * P], U8, name="planes", align_bytes=256)
-            values = grouped[:].rearrange("p g m u -> p (g m u)").bitcast(BF16)
-            half = ROUND_GROUPS * P // 2
-            for h in range(2):
+        def quantise_piece(r):
+            n = CHUNK_GROUPS[PIECES[r][0]]
+            codes[r] = code_pool.tile([P, n * P], U32, name="codes", align_bytes=256)
+            planes[r] = code_pool.tile([P, n * P], U8, name="planes", align_bytes=256)
+            values = grouped[r][:].rearrange("p g m u -> p (g m u)").bitcast(BF16)
+            width = min(n, QUANT_GROUPS) * P
+            for w0 in range(0, n * P, width):
                 nc.vector.quantize_mx(
-                    out=codes[r][:, h * half : (h + 1) * half].bitcast(FP8X4),
-                    scales=planes[r][:, h * half : (h + 1) * half],
-                    in_=values[:, 4 * h * half : 4 * (h + 1) * half],
+                    out=codes[r][:, w0 : w0 + width].bitcast(FP8X4),
+                    scales=planes[r][:, w0 : w0 + width],
+                    in_=values[:, 4 * w0 : 4 * (w0 + width)],
                 )
 
-        def multiply_round(r):
-            c, b = ORDER[r]
-            round_codes = codes[r]
-            round_planes = planes[r]
-            for j in range(ROUND_GROUPS):
-                g = c * ROUND_GROUPS + j
+        def multiply_piece(r):
+            c, b = PIECES[r]
+            for j in range(CHUNK_GROUPS[c]):
+                g = CHUNK_START[c] + j
                 nc.tensor.matmul_mx(
                     out=sums[b][:],
-                    lhsT=round_codes[:, j * P : (j + 1) * P].bitcast(FP8X4),
-                    lhsT_scale=round_planes[:, j * P : (j + 1) * P],
+                    lhsT=codes[r][:, j * P : (j + 1) * P].bitcast(FP8X4),
+                    lhsT_scale=planes[r][:, j * P : (j + 1) * P],
                     rhs=w_words[c][:, j, :].bitcast(FP4X4),
                     rhs_scale=w_planes[c][:, j, :],
                     start=(g == 0),
@@ -137,7 +156,6 @@ def tile_ufoattention_pb_k_kernel(tc, queries, Wq_words, Wq_scales, bq, gamma, o
                 )
 
         q_sb = {}
-        squares = {}
         norm2 = {}
 
         def add_bias(b, h0=0, h1=HEADS):
@@ -150,14 +168,13 @@ def tile_ufoattention_pb_k_kernel(tc, queries, Wq_words, Wq_scales, bq, gamma, o
                 op=ADD,
             )
 
-
-        def square(b):
-            squares[b] = end_pool.tile([P, HEADS, HEAD_DIM], F32, name="squares")
-            nc.scalar.activation(out=squares[b][:], in_=q_sb[b][:], func=ACT.Square)
-
         def sum_squares(b):
             norm2[b] = end_pool.tile([P, HEADS], F32, name="norm2")
-            nc.vector.tensor_reduce(out=norm2[b][:], in_=squares[b][:], axis=mybir.AxisListType.X, op=ADD)
+            waste = end_pool.tile([P, HEADS, HEAD_DIM], F32, name="waste")
+            for h in range(HEADS):
+                nc.scalar.activation(
+                    out=waste[:, h, :], in_=q_sb[b][:, h, :], func=ACT.Square, accum_out=norm2[b][:, h : h + 1]
+                )
 
         def scale_and_store(b):
             norm = end_pool.tile([P, HEADS], F32, name="norm")
@@ -178,7 +195,7 @@ def tile_ufoattention_pb_k_kernel(tc, queries, Wq_words, Wq_scales, bq, gamma, o
             halves = [(0, half), (half, HEADS)]
             for h0, h1 in halves:
                 add_bias(b, h0, h1)
-            scaled = end_pool.tile([P, HEADS, HEAD_DIM], F32, name="squares")
+            scaled = end_pool.tile([P, HEADS, HEAD_DIM], F32, name="scaled")
             norm_sum = end_pool.tile([P, HEADS], F32, name="norm2")
             norm = end_pool.tile([P, HEADS], F32, name="norm")
             inverse = end_pool.tile([P, HEADS], F32, name="inverse")
@@ -206,28 +223,56 @@ def tile_ufoattention_pb_k_kernel(tc, queries, Wq_words, Wq_scales, bq, gamma, o
                 )
                 nc.sync.dma_start(out=out[b, h0:h1].rearrange("h n d -> n h d"), in_=result[:, h0:h1, :])
 
-        for r in range(RAW_BUFS):
-            load_round(r)
+        pieces = len(PIECES)
+        first_full = CHUNK_GROUPS.index(MAX_GROUPS) * BATCHES
+        loaded = 0
+        cleared = 2
 
-        for i in range(-2, ROUNDS):
-            ended = [ORDER[i - 1][1]] if i >= 1 and ORDER[i - 1][0] == CHUNKS - 1 and ORDER[i - 1][1] != LAST else []
-            for b in ended:
+        def load_next():
+            c, b = PIECES[loaded]
+            load_piece(loaded)
+            if loaded == pieces - 1:
+                nc.sync.dma_start(out=bias[:].rearrange("p h d -> p (h d)"), in_=bq.partition_broadcast(P))
+                nc.sync.dma_start(out=gains[:], in_=gamma.rearrange("a h b c -> (a h b c)").partition_broadcast(P))
+
+        runs = []
+        for count in RUN_PIECES:
+            start = sum(len(run) for run in runs)
+            runs.append(range(start, start + count))
+        while loaded < first_full:
+            load_next()
+            loaded += 1
+
+        done = []
+        sorted_runs = 0
+        for i in range(-2, len(runs)):
+            for b in done:
                 add_bias(b)
-            if i + 2 < ROUNDS:
-                sort_round(i + 2)
-                if i + 2 + RAW_BUFS < ROUNDS:
-                    load_round(i + 2 + RAW_BUFS)
-                if i + 2 + RAW_BUFS == ROUNDS:
-                    nc.sync.dma_start(out=bias[:].rearrange("p h d -> p (h d)"), in_=bq.partition_broadcast(P))
-                    nc.sync.dma_start(
-                        out=gains[:], in_=gamma.rearrange("a h b c -> (a h b c)").partition_broadcast(P)
-                    )
-            if 0 <= i + 1 < ROUNDS:
-                quantise_round(i + 1, transpose_round(i + 1))
-            for b in ended:
-                square(b)
+            ahead = min(i + (2 if i < DEEPER else 3), len(runs) - 1)
+            while sorted_runs <= ahead:
+                for r in runs[sorted_runs]:
+                    sort_piece(r)
+                sorted_runs += 1
+            if 0 <= i + 1 < len(runs):
+                for r in runs[i + 1]:
+                    flip_piece(r)
+                for r in runs[i + 1]:
+                    quantise_piece(r)
+            for b in done:
                 sum_squares(b)
                 scale_and_store(b)
-            if 0 <= i < ROUNDS:
-                multiply_round(i)
+            done = []
+            if i >= 0:
+                for r in runs[i]:
+                    multiply_piece(r)
+                    c, b = PIECES[r]
+                    if c == CHUNKS - 1 and b != LAST:
+                        done.append(b)
+            sorted_to = runs[sorted_runs - 1].stop
+            for r in range(loaded, min(loaded + 2, pieces, max(first_full, sorted_to) + RAW_BUFS)):
+                if PIECES[r] == (cleared, 0):
+                    clear_planes(cleared)
+                    cleared += 1
+                load_next()
+                loaded += 1
         end_last_batch()

@@ -30,6 +30,10 @@ KEPT_BACK = [(c, LAST) for c in range(CHUNKS - 2, CHUNKS)]
 PIECES = [(c, b) for c in range(CHUNKS) for b in range(BATCHES) if (c, b) not in KEPT_BACK] + KEPT_BACK
 RUN_PIECES = [1] * 4 + [2] * 2 + [1] * 12
 DEEPER = 8
+QUARTERS = 4
+QUARTER = N_OUT // QUARTERS
+QUARTER_HEADS = HEADS // QUARTERS
+HALF_HEADS = HEADS // 2
 BANK_GROUPS = 2
 FLIP_BANKS = 4
 MAX_GROUPS = max(CHUNK_GROUPS)
@@ -54,7 +58,7 @@ def tile_ufoattention_pb_k_kernel(tc, queries, Wq_words, Wq_scales, bq, gamma, o
 
         w_words = [keep.tile([P, g, 2 * N_OUT], U8, name="w_words%d" % c, align_bytes=256) for c, g in enumerate(CHUNK_GROUPS)]
         w_planes = [keep.tile([P, g, N_OUT], U8, name="w_planes%d" % c, align_bytes=256) for c, g in enumerate(CHUNK_GROUPS)]
-        ident = keep.tile([P, P], F32)
+        ident = keep.tile([P, P], F32, align_bytes=256)
         bias = keep.tile([P, HEADS, HEAD_DIM], BF16)
         gains = keep.tile([P, HEADS], BF16)
         one = keep.tile([P, 1], F32)
@@ -92,9 +96,9 @@ def tile_ufoattention_pb_k_kernel(tc, queries, Wq_words, Wq_scales, bq, gamma, o
             c, b = PIECES[r]
             n = CHUNK_GROUPS[c]
             if n == MAX_GROUPS:
-                raw[r] = raw_pool.tile([P, n * K_GROUP], BF16, name="raw")
+                raw[r] = raw_pool.tile([P, n * K_GROUP], BF16, name="raw", align_bytes=256)
             else:
-                raw[r] = keep.tile([P, n * K_GROUP], BF16, name="raw_%d_%d" % (c, b))
+                raw[r] = keep.tile([P, n * K_GROUP], BF16, name="raw_%d_%d" % (c, b), align_bytes=256)
             k0 = CHUNK_START[c] * K_GROUP
             part = n * K_GROUP // (2 if r == 0 else 1)
             for start in range(0, n * K_GROUP, part):
@@ -106,7 +110,7 @@ def tile_ufoattention_pb_k_kernel(tc, queries, Wq_words, Wq_scales, bq, gamma, o
 
         def sort_piece(r):
             n = CHUNK_GROUPS[PIECES[r][0]]
-            sorted_words[r] = sort_pool.tile([P, n, 2, P], F32, name="sorted_words")
+            sorted_words[r] = sort_pool.tile([P, n, 2, P], F32, name="sorted_words", align_bytes=256)
             words = raw[r][:].bitcast(F32).rearrange("m (g p u) -> m g u p", g=n, u=2)
             part = n // (2 if r == 0 else 1)
             for start in range(0, n, part):
@@ -143,6 +147,7 @@ def tile_ufoattention_pb_k_kernel(tc, queries, Wq_words, Wq_scales, bq, gamma, o
 
         def multiply_piece(r):
             c, b = PIECES[r]
+            last_pass = GROUPS - 1 if b != LAST else GROUPS - 1 - CHUNK_GROUPS[-1]
             for j in range(CHUNK_GROUPS[c]):
                 g = CHUNK_START[c] + j
                 nc.tensor.matmul_mx(
@@ -152,20 +157,33 @@ def tile_ufoattention_pb_k_kernel(tc, queries, Wq_words, Wq_scales, bq, gamma, o
                     rhs=w_words[c][:, j, :].bitcast(FP4X4),
                     rhs_scale=w_planes[c][:, j, :],
                     start=(g == 0),
-                    stop=(g == GROUPS - 1),
+                    stop=(g == last_pass),
                 )
+
+        def multiply_quarter(r, quarter):
+            c, b = PIECES[r]
+            cols = slice(quarter * QUARTER, (quarter + 1) * QUARTER)
+            quarter_sums = flip_psum.tile([P, QUARTER_HEADS, HEAD_DIM], F32, name="flipped")
+            for j in range(CHUNK_GROUPS[c]):
+                nc.tensor.matmul_mx(
+                    out=quarter_sums[:].rearrange("p h d -> p (h d)"),
+                    lhsT=codes[r][:, j * P : (j + 1) * P].bitcast(FP8X4),
+                    lhsT_scale=planes[r][:, j * P : (j + 1) * P],
+                    rhs=w_words[c][:, j, 2 * quarter * QUARTER : 2 * (quarter + 1) * QUARTER].bitcast(FP4X4),
+                    rhs_scale=w_planes[c][:, j, cols],
+                    start=(j == 0),
+                    stop=(j == CHUNK_GROUPS[c] - 1),
+                )
+            return quarter_sums
 
         q_sb = {}
         norm2 = {}
+        norms = {}
 
-        def add_bias(b, h0=0, h1=HEADS):
-            if h0 == 0:
-                q_sb[b] = end_pool.tile([P, HEADS, HEAD_DIM], F32, name="q_sb")
+        def add_bias(b):
+            q_sb[b] = end_pool.tile([P, HEADS, HEAD_DIM], F32, name="q_sb")
             nc.vector.tensor_tensor(
-                out=q_sb[b][:, h0:h1, :],
-                in0=sums[b][:].rearrange("p (h d) -> p h d", h=HEADS)[:, h0:h1, :],
-                in1=bias[:, h0:h1, :],
-                op=ADD,
+                out=q_sb[b][:], in0=sums[b][:].rearrange("p (h d) -> p h d", h=HEADS), in1=bias[:], op=ADD
             )
 
         def sum_squares(b):
@@ -176,52 +194,63 @@ def tile_ufoattention_pb_k_kernel(tc, queries, Wq_words, Wq_scales, bq, gamma, o
                     out=waste[:, h, :], in_=q_sb[b][:, h, :], func=ACT.Square, accum_out=norm2[b][:, h : h + 1]
                 )
 
-        def scale_and_store(b):
-            norm = end_pool.tile([P, HEADS], F32, name="norm")
-            nc.scalar.activation(out=norm[:], in_=norm2[b][:], func=ACT.Sqrt)
+            norms[b] = end_pool.tile([P, HEADS], F32, name="norm")
+            nc.scalar.activation(out=norms[b][:], in_=norm2[b][:], func=ACT.Sqrt)
+
+        def scale_and_store(b, engine):
             inverse = end_pool.tile([P, HEADS], F32, name="inverse")
-            nc.vector.reciprocal(out=inverse[:], in_=norm[:])
+            nc.vector.reciprocal(out=inverse[:], in_=norms[b][:])
             factor = end_pool.tile([P, HEADS], F32, name="factor")
             nc.vector.tensor_tensor(out=factor[:], in0=inverse[:], in1=gains[:], op=MULT)
             result = end_pool.tile([P, HEADS, HEAD_DIM], F32, name="result")
-            nc.vector.tensor_tensor(
+            engine.tensor_tensor(
                 out=result[:], in0=q_sb[b][:], in1=factor[:].unsqueeze(2).to_broadcast([P, HEADS, HEAD_DIM]), op=MULT
             )
             nc.sync.dma_start(out=out[b].rearrange("h n d -> n h d"), in_=result[:])
 
-        def end_last_batch():
-            b = LAST
-            half = HEADS // 2
-            halves = [(0, half), (half, HEADS)]
-            for h0, h1 in halves:
-                add_bias(b, h0, h1)
-            scaled = end_pool.tile([P, HEADS, HEAD_DIM], F32, name="scaled")
+        def finish_last_batch(unfinished):
+            r = len(PIECES) - 1
+            add_bias(LAST)
+            for b in unfinished:
+                scale_and_store(b, nc.gpsimd)
+            q = keep.tile([P, HEADS, HEAD_DIM], F32, name="q_last")
+            waste = end_pool.tile([P, HEADS, HEAD_DIM], F32, name="waste")
             norm_sum = end_pool.tile([P, HEADS], F32, name="norm2")
             norm = end_pool.tile([P, HEADS], F32, name="norm")
             inverse = end_pool.tile([P, HEADS], F32, name="inverse")
             result = end_pool.tile([P, HEADS, HEAD_DIM], F32, name="result")
-            waste = end_pool.tile([P, HEADS, HEAD_DIM], F32, name="waste")
-            for h0, h1 in halves:
-                for h in range(h0, h1):
-                    nc.scalar.activation(
-                        out=waste[:, h, :], in_=q_sb[b][:, h, :], func=ACT.Square, accum_out=norm_sum[:, h : h + 1]
-                    )
-                nc.scalar.activation(out=norm[:, h0:h1], in_=norm_sum[:, h0:h1], func=ACT.Sqrt)
-                nc.vector.tensor_tensor(
-                    out=scaled[:, h0:h1, :],
-                    in0=q_sb[b][:, h0:h1, :],
-                    in1=gains[:, h0:h1].unsqueeze(2).to_broadcast([P, h1 - h0, HEAD_DIM]),
-                    op=MULT,
-                )
-            for h0, h1 in halves:
+            factor = end_pool.tile([P, HEADS], F32, name="factor")
+
+            def finish_half(half):
+                h0, h1 = half * HALF_HEADS, (half + 1) * HALF_HEADS
                 nc.vector.reciprocal(out=inverse[:, h0:h1], in_=norm[:, h0:h1])
+                nc.vector.tensor_tensor(out=factor[:, h0:h1], in0=inverse[:, h0:h1], in1=gains[:, h0:h1], op=MULT)
                 nc.vector.tensor_tensor(
                     out=result[:, h0:h1, :],
-                    in0=scaled[:, h0:h1, :],
-                    in1=inverse[:, h0:h1].unsqueeze(2).to_broadcast([P, h1 - h0, HEAD_DIM]),
+                    in0=q[:, h0:h1, :],
+                    in1=factor[:, h0:h1].unsqueeze(2).to_broadcast([P, HALF_HEADS, HEAD_DIM]),
                     op=MULT,
                 )
-                nc.sync.dma_start(out=out[b, h0:h1].rearrange("h n d -> n h d"), in_=result[:, h0:h1, :])
+                nc.sync.dma_start(out=out[LAST, h0:h1].rearrange("h n d -> n h d"), in_=result[:, h0:h1, :])
+
+            for quarter in range(QUARTERS):
+                quarter_sums = multiply_quarter(r, quarter)
+                h0, h1 = quarter * QUARTER_HEADS, (quarter + 1) * QUARTER_HEADS
+                nc.vector.tensor_tensor(
+                    out=q[:, h0:h1, :],
+                    in0=quarter_sums[:],
+                    in1=q_sb[LAST][:, h0:h1, :],
+                    op=ADD,
+                )
+                for h in range(h0, h1):
+                    nc.scalar.activation(
+                        out=waste[:, h, :], in_=q[:, h, :], func=ACT.Square, accum_out=norm_sum[:, h : h + 1]
+                    )
+                if h1 % HALF_HEADS == 0:
+                    half = slice(h1 - HALF_HEADS, h1)
+                    nc.scalar.activation(out=norm[:, half], in_=norm_sum[:, half], func=ACT.Sqrt)
+            finish_half(0)
+            finish_half(1)
 
         pieces = len(PIECES)
         first_full = CHUNK_GROUPS.index(MAX_GROUPS) * BATCHES
@@ -244,6 +273,7 @@ def tile_ufoattention_pb_k_kernel(tc, queries, Wq_words, Wq_scales, bq, gamma, o
             loaded += 1
 
         done = []
+        unfinished = []
         sorted_runs = 0
         for i in range(-2, len(runs)):
             for b in done:
@@ -260,9 +290,12 @@ def tile_ufoattention_pb_k_kernel(tc, queries, Wq_words, Wq_scales, bq, gamma, o
                     quantise_piece(r)
             for b in done:
                 sum_squares(b)
-                scale_and_store(b)
+                if i == len(runs) - 2:
+                    unfinished.append(b)
+                else:
+                    scale_and_store(b, nc.vector)
             done = []
-            if i >= 0:
+            if 0 <= i < len(runs) - 1:
                 for r in runs[i]:
                     multiply_piece(r)
                     c, b = PIECES[r]
@@ -275,4 +308,4 @@ def tile_ufoattention_pb_k_kernel(tc, queries, Wq_words, Wq_scales, bq, gamma, o
                     cleared += 1
                 load_next()
                 loaded += 1
-        end_last_batch()
+        finish_last_batch(unfinished)

@@ -28,7 +28,7 @@ CHUNK_START = [sum(CHUNK_GROUPS[:c]) for c in range(CHUNKS)]
 LAST = BATCHES - 1
 KEPT_BACK = [(c, LAST) for c in range(CHUNKS - 2, CHUNKS)]
 PIECES = [(c, b) for c in range(CHUNKS) for b in range(BATCHES) if (c, b) not in KEPT_BACK] + KEPT_BACK
-RUN_PIECES = [1] * 4 + [2] * 2 + [1] * 12
+RUN_PIECES = [1] * 2 + [2] * 3 + [1] * 12
 DEEPER = 8
 QUARTERS = 4
 QUARTER = N_OUT // QUARTERS
@@ -76,7 +76,7 @@ def tile_ufoattention_pb_k_kernel(tc, queries, Wq_words, Wq_scales, bq, gamma, o
         for c in range(2):
             clear_planes(c)
         make_identity(nc, ident[:])
-        nc.scalar.activation(out=one_root[:], in_=one[:], func=ACT.Sqrt)
+        nc.scalar.activation(out=one_root[:], in_=one[:], func=ACT.Abs_reciprocal_sqrt)
 
         raw = {}
         sorted_words = {}
@@ -178,7 +178,7 @@ def tile_ufoattention_pb_k_kernel(tc, queries, Wq_words, Wq_scales, bq, gamma, o
 
         q_sb = {}
         norm2 = {}
-        norms = {}
+        inverses = {}
 
         def add_bias(b):
             q_sb[b] = end_pool.tile([P, HEADS, HEAD_DIM], F32, name="q_sb")
@@ -194,14 +194,12 @@ def tile_ufoattention_pb_k_kernel(tc, queries, Wq_words, Wq_scales, bq, gamma, o
                     out=waste[:, h, :], in_=q_sb[b][:, h, :], func=ACT.Square, accum_out=norm2[b][:, h : h + 1]
                 )
 
-            norms[b] = end_pool.tile([P, HEADS], F32, name="norm")
-            nc.scalar.activation(out=norms[b][:], in_=norm2[b][:], func=ACT.Sqrt)
+            inverses[b] = end_pool.tile([P, HEADS], F32, name="inverse")
+            nc.scalar.activation(out=inverses[b][:], in_=norm2[b][:], func=ACT.Abs_reciprocal_sqrt)
 
         def scale_and_store(b, engine):
-            inverse = end_pool.tile([P, HEADS], F32, name="inverse")
-            nc.vector.reciprocal(out=inverse[:], in_=norms[b][:])
             factor = end_pool.tile([P, HEADS], F32, name="factor")
-            nc.vector.tensor_tensor(out=factor[:], in0=inverse[:], in1=gains[:], op=MULT)
+            nc.vector.tensor_tensor(out=factor[:], in0=inverses[b][:], in1=gains[:], op=MULT)
             result = end_pool.tile([P, HEADS, HEAD_DIM], F32, name="result")
             engine.tensor_tensor(
                 out=result[:], in0=q_sb[b][:], in1=factor[:].unsqueeze(2).to_broadcast([P, HEADS, HEAD_DIM]), op=MULT
@@ -216,14 +214,12 @@ def tile_ufoattention_pb_k_kernel(tc, queries, Wq_words, Wq_scales, bq, gamma, o
             q = keep.tile([P, HEADS, HEAD_DIM], F32, name="q_last")
             waste = end_pool.tile([P, HEADS, HEAD_DIM], F32, name="waste")
             norm_sum = end_pool.tile([P, HEADS], F32, name="norm2")
-            norm = end_pool.tile([P, HEADS], F32, name="norm")
             inverse = end_pool.tile([P, HEADS], F32, name="inverse")
             result = end_pool.tile([P, HEADS, HEAD_DIM], F32, name="result")
             factor = end_pool.tile([P, HEADS], F32, name="factor")
 
             def finish_half(half):
                 h0, h1 = half * HALF_HEADS, (half + 1) * HALF_HEADS
-                nc.vector.reciprocal(out=inverse[:, h0:h1], in_=norm[:, h0:h1])
                 nc.vector.tensor_tensor(out=factor[:, h0:h1], in0=inverse[:, h0:h1], in1=gains[:, h0:h1], op=MULT)
                 nc.vector.tensor_tensor(
                     out=result[:, h0:h1, :],
@@ -248,7 +244,7 @@ def tile_ufoattention_pb_k_kernel(tc, queries, Wq_words, Wq_scales, bq, gamma, o
                     )
                 if h1 % HALF_HEADS == 0:
                     half = slice(h1 - HALF_HEADS, h1)
-                    nc.scalar.activation(out=norm[:, half], in_=norm_sum[:, half], func=ACT.Sqrt)
+                    nc.scalar.activation(out=inverse[:, half], in_=norm_sum[:, half], func=ACT.Abs_reciprocal_sqrt)
             finish_half(0)
             finish_half(1)
 

@@ -197,20 +197,25 @@ def tile_ufoattention_pb_k_kernel(tc, queries, Wq_words, Wq_scales, bq, gamma, o
             inverses[b] = end_pool.tile([P, HEADS], F32, name="inverse")
             nc.scalar.activation(out=inverses[b][:], in_=norm2[b][:], func=ACT.Abs_reciprocal_sqrt)
 
-        def scale_and_store(b, engine):
+        def scale_and_store(b, engine, step):
             factor = end_pool.tile([P, HEADS], F32, name="factor")
             nc.vector.tensor_tensor(out=factor[:], in0=inverses[b][:], in1=gains[:], op=MULT)
             result = end_pool.tile([P, HEADS, HEAD_DIM], F32, name="result")
-            engine.tensor_tensor(
-                out=result[:], in0=q_sb[b][:], in1=factor[:].unsqueeze(2).to_broadcast([P, HEADS, HEAD_DIM]), op=MULT
-            )
-            nc.sync.dma_start(out=out[b].rearrange("h n d -> n h d"), in_=result[:])
+            for h0 in range(0, HEADS, step):
+                heads = slice(h0, h0 + step)
+                engine.tensor_tensor(
+                    out=result[:, heads, :],
+                    in0=q_sb[b][:, heads, :],
+                    in1=factor[:, heads].unsqueeze(2).to_broadcast([P, step, HEAD_DIM]),
+                    op=MULT,
+                )
+                nc.sync.dma_start(out=out[b, heads].rearrange("h n d -> n h d"), in_=result[:, heads, :])
 
         def finish_last_batch(unfinished):
             r = len(PIECES) - 1
-            add_bias(LAST)
             for b in unfinished:
-                scale_and_store(b, nc.gpsimd)
+                scale_and_store(b, nc.gpsimd, HALF_HEADS)
+            add_bias(LAST)
             q = keep.tile([P, HEADS, HEAD_DIM], F32, name="q_last")
             waste = end_pool.tile([P, HEADS, HEAD_DIM], F32, name="waste")
             norm_sum = end_pool.tile([P, HEADS], F32, name="norm2")
@@ -218,15 +223,28 @@ def tile_ufoattention_pb_k_kernel(tc, queries, Wq_words, Wq_scales, bq, gamma, o
             result = end_pool.tile([P, HEADS, HEAD_DIM], F32, name="result")
             factor = end_pool.tile([P, HEADS], F32, name="factor")
 
-            def finish_half(half):
-                h0, h1 = half * HALF_HEADS, (half + 1) * HALF_HEADS
-                nc.vector.tensor_tensor(out=factor[:, h0:h1], in0=inverse[:, h0:h1], in1=gains[:, h0:h1], op=MULT)
+            def finish_first_half():
+                heads = slice(0, HALF_HEADS)
+                nc.vector.tensor_tensor(out=factor[:, heads], in0=inverse[:, heads], in1=gains[:, heads], op=MULT)
                 nc.vector.tensor_tensor(
-                    out=result[:, h0:h1, :],
-                    in0=q[:, h0:h1, :],
-                    in1=factor[:, h0:h1].unsqueeze(2).to_broadcast([P, HALF_HEADS, HEAD_DIM]),
+                    out=result[:, heads, :],
+                    in0=q[:, heads, :],
+                    in1=factor[:, heads].unsqueeze(2).to_broadcast([P, HALF_HEADS, HEAD_DIM]),
                     op=MULT,
                 )
+                nc.sync.dma_start(out=out[LAST, heads].rearrange("h n d -> n h d"), in_=result[:, heads, :])
+
+            def finish_quarter(quarter):
+                h0, h1 = quarter * QUARTER_HEADS, (quarter + 1) * QUARTER_HEADS
+                for h in range(h0, h1):
+                    nc.vector.scalar_tensor_tensor(
+                        out=result[:, h, :],
+                        in0=q[:, h, :],
+                        scalar=inverse[:, h : h + 1],
+                        in1=gains[:, h : h + 1].to_broadcast([P, HEAD_DIM]),
+                        op0=MULT,
+                        op1=MULT,
+                    )
                 nc.sync.dma_start(out=out[LAST, h0:h1].rearrange("h n d -> n h d"), in_=result[:, h0:h1, :])
 
             for quarter in range(QUARTERS):
@@ -245,8 +263,9 @@ def tile_ufoattention_pb_k_kernel(tc, queries, Wq_words, Wq_scales, bq, gamma, o
                 if h1 % HALF_HEADS == 0:
                     half = slice(h1 - HALF_HEADS, h1)
                     nc.scalar.activation(out=inverse[:, half], in_=norm_sum[:, half], func=ACT.Abs_reciprocal_sqrt)
-            finish_half(0)
-            finish_half(1)
+            finish_first_half()
+            finish_quarter(2)
+            finish_quarter(3)
 
         pieces = len(PIECES)
         first_full = CHUNK_GROUPS.index(MAX_GROUPS) * BATCHES
@@ -289,7 +308,7 @@ def tile_ufoattention_pb_k_kernel(tc, queries, Wq_words, Wq_scales, bq, gamma, o
                 if i == len(runs) - 2:
                     unfinished.append(b)
                 else:
-                    scale_and_store(b, nc.vector)
+                    scale_and_store(b, nc.vector, HEADS)
             done = []
             if 0 <= i < len(runs) - 1:
                 for r in runs[i]:

from contextlib import ExitStack

import concourse.mybir as mybir
from concourse.masks import make_identity

F32 = mybir.dt.float32
BF16 = mybir.dt.bfloat16
I32 = mybir.dt.int32
U32 = mybir.dt.uint32
U8 = mybir.dt.uint8
FP8X4 = mybir.dt.float8_e4m3fn_x4
FP4X4 = mybir.dt.float4_e2m1fn_x4
ADD = mybir.AluOpType.add
MULT = mybir.AluOpType.mult
ACT = mybir.ActivationFunctionType

P = 128
BATCHES = 4
D = 16384
HEADS = 8
HEAD_DIM = 64
N_OUT = HEADS * HEAD_DIM
K_GROUP = 512
GROUPS = D // K_GROUP
CHUNK_GROUPS = [4, 4, 8, 8, 8]
CHUNKS = len(CHUNK_GROUPS)
CHUNK_START = [sum(CHUNK_GROUPS[:c]) for c in range(CHUNKS)]
LAST = BATCHES - 1
KEPT_BACK = [(c, LAST) for c in range(CHUNKS - 2, CHUNKS)]
PIECES = [(c, b) for c in range(CHUNKS) for b in range(BATCHES) if (c, b) not in KEPT_BACK] + KEPT_BACK
RUN_PIECES = [1] * 2 + [2] * 3 + [1] * 12
DEEPER = 8
QUARTERS = 4
QUARTER = N_OUT // QUARTERS
QUARTER_HEADS = HEADS // QUARTERS
HALF_HEADS = HEADS // 2
BANK_GROUPS = 2
FLIP_BANKS = 4
MAX_GROUPS = max(CHUNK_GROUPS)
RAW_BUFS = 7
QUANT_GROUPS = 4

FLOPS = 2 * BATCHES * P * D * N_OUT


def tile_ufoattention_pb_k_kernel(tc, queries, Wq_words, Wq_scales, bq, gamma, out):
    nc = tc.nc
    with ExitStack() as ctx:
        ctx.enter_context(tc.manual_schedule())
        keep = ctx.enter_context(tc.tile_pool(name="keep", bufs=1))
        raw_pool = ctx.enter_context(tc.tile_pool(name="raw", bufs=RAW_BUFS))
        sort_pool = ctx.enter_context(tc.tile_pool(name="sort", bufs=4))
        group_pool = ctx.enter_context(tc.tile_pool(name="group", bufs=2))
        code_pool = ctx.enter_context(tc.tile_pool(name="code", bufs=4))
        end_pool = ctx.enter_context(tc.tile_pool(name="end", bufs=2))
        sum_psum = ctx.enter_context(tc.psum_pool(name="sums", bufs=1))
        flip_psum = ctx.enter_context(tc.psum_pool(name="flip", bufs=FLIP_BANKS))

        w_words = [keep.tile([P, g, 2 * N_OUT], U8, name="w_words%d" % c, align_bytes=256) for c, g in enumerate(CHUNK_GROUPS)]
        w_planes = [keep.tile([P, g, N_OUT], U8, name="w_planes%d" % c, align_bytes=256) for c, g in enumerate(CHUNK_GROUPS)]
        ident = keep.tile([P, P], F32, align_bytes=256)
        bias = keep.tile([P, HEADS, HEAD_DIM], BF16)
        gains = keep.tile([P, HEADS], BF16)
        one = keep.tile([P, 1], F32)
        one_root = keep.tile([P, 1], F32)
        sums = [sum_psum.tile([P, N_OUT], F32, name="sums%d" % b) for b in range(BATCHES)]

        words_dram = Wq_words.bitcast(I32)
        scales_dram = Wq_scales.bitcast(I32).rearrange("g (Q r) n -> r Q g n", r=4)

        nc.vector.memset(one[:], 1.0)

        def clear_planes(c):
            nc.vector.memset(w_planes[c][:].bitcast(I32), 0)

        for c in range(2):
            clear_planes(c)
        make_identity(nc, ident[:])
        nc.scalar.activation(out=one_root[:], in_=one[:], func=ACT.Abs_reciprocal_sqrt)

        raw = {}
        sorted_words = {}
        grouped = {}
        codes = {}
        planes = {}

        def load_weights(c):
            chunk = slice(CHUNK_START[c], CHUNK_START[c] + CHUNK_GROUPS[c])
            for r in range(4):
                nc.sync.dma_start(out=w_planes[c][r:P:32, :, :].bitcast(I32), in_=scales_dram[r, :, chunk, :])
            nc.sync.dma_start(
                out=w_words[c][:].bitcast(I32), in_=words_dram[chunk].rearrange("g p n -> p g n")
            )

        def load_piece(r):
            c, b = PIECES[r]
            n = CHUNK_GROUPS[c]
            if n == MAX_GROUPS:
                raw[r] = raw_pool.tile([P, n * K_GROUP], BF16, name="raw", align_bytes=256)
            else:
                raw[r] = keep.tile([P, n * K_GROUP], BF16, name="raw_%d_%d" % (c, b), align_bytes=256)
            k0 = CHUNK_START[c] * K_GROUP
            part = n * K_GROUP // (2 if r == 0 else 1)
            for start in range(0, n * K_GROUP, part):
                nc.sync.dma_start(
                    out=raw[r][:, start : start + part], in_=queries[b, :, k0 + start : k0 + start + part]
                )
            if b == 1:
                load_weights(c)

        def sort_piece(r):
            n = CHUNK_GROUPS[PIECES[r][0]]
            sorted_words[r] = sort_pool.tile([P, n, 2, P], F32, name="sorted_words", align_bytes=256)
            words = raw[r][:].bitcast(F32).rearrange("m (g p u) -> m g u p", g=n, u=2)
            part = n // (2 if r == 0 else 1)
            for start in range(0, n, part):
                nc.vector.tensor_copy(
                    out=sorted_words[r][:, start : start + part, :, :], in_=words[:, start : start + part, :, :]
                )

        def flip_piece(r):
            n = CHUNK_GROUPS[PIECES[r][0]]
            grouped[r] = group_pool.tile([P, n, P, 2], F32, name="grouped", align_bytes=256)
            source = sorted_words[r]
            for bank in range(n // BANK_GROUPS):
                flipped = flip_psum.tile([P, BANK_GROUPS, 2, P], F32, name="flipped")
                for j in range(BANK_GROUPS):
                    for u in range(2):
                        nc.tensor.transpose(flipped[:, j, u, :], source[:, bank * BANK_GROUPS + j, u, :], ident[:])
                nc.scalar.copy(
                    out=grouped[r][:, bank * BANK_GROUPS : (bank + 1) * BANK_GROUPS, :, :],
                    in_=flipped[:].rearrange("p j u m -> p j m u"),
                )

        def quantise_piece(r):
            n = CHUNK_GROUPS[PIECES[r][0]]
            codes[r] = code_pool.tile([P, n * P], U32, name="codes", align_bytes=256)
            planes[r] = code_pool.tile([P, n * P], U8, name="planes", align_bytes=256)
            values = grouped[r][:].rearrange("p g m u -> p (g m u)").bitcast(BF16)
            width = min(n, QUANT_GROUPS) * P
            for w0 in range(0, n * P, width):
                nc.vector.quantize_mx(
                    out=codes[r][:, w0 : w0 + width].bitcast(FP8X4),
                    scales=planes[r][:, w0 : w0 + width],
                    in_=values[:, 4 * w0 : 4 * (w0 + width)],
                )

        def multiply_piece(r):
            c, b = PIECES[r]
            last_pass = GROUPS - 1 if b != LAST else GROUPS - 1 - CHUNK_GROUPS[-1]
            for j in range(CHUNK_GROUPS[c]):
                g = CHUNK_START[c] + j
                nc.tensor.matmul_mx(
                    out=sums[b][:],
                    lhsT=codes[r][:, j * P : (j + 1) * P].bitcast(FP8X4),
                    lhsT_scale=planes[r][:, j * P : (j + 1) * P],
                    rhs=w_words[c][:, j, :].bitcast(FP4X4),
                    rhs_scale=w_planes[c][:, j, :],
                    start=(g == 0),
                    stop=(g == last_pass),
                )

        def multiply_quarter(r, quarter):
            c, b = PIECES[r]
            cols = slice(quarter * QUARTER, (quarter + 1) * QUARTER)
            quarter_sums = flip_psum.tile([P, QUARTER_HEADS, HEAD_DIM], F32, name="flipped")
            for j in range(CHUNK_GROUPS[c]):
                nc.tensor.matmul_mx(
                    out=quarter_sums[:].rearrange("p h d -> p (h d)"),
                    lhsT=codes[r][:, j * P : (j + 1) * P].bitcast(FP8X4),
                    lhsT_scale=planes[r][:, j * P : (j + 1) * P],
                    rhs=w_words[c][:, j, 2 * quarter * QUARTER : 2 * (quarter + 1) * QUARTER].bitcast(FP4X4),
                    rhs_scale=w_planes[c][:, j, cols],
                    start=(j == 0),
                    stop=(j == CHUNK_GROUPS[c] - 1),
                )
            return quarter_sums

        q_sb = {}
        norm2 = {}
        inverses = {}

        def add_bias(b):
            q_sb[b] = end_pool.tile([P, HEADS, HEAD_DIM], F32, name="q_sb")
            nc.vector.tensor_tensor(
                out=q_sb[b][:], in0=sums[b][:].rearrange("p (h d) -> p h d", h=HEADS), in1=bias[:], op=ADD
            )

        def sum_squares(b):
            norm2[b] = end_pool.tile([P, HEADS], F32, name="norm2")
            waste = end_pool.tile([P, HEADS, HEAD_DIM], F32, name="waste")
            for h in range(HEADS):
                nc.scalar.activation(
                    out=waste[:, h, :], in_=q_sb[b][:, h, :], func=ACT.Square, accum_out=norm2[b][:, h : h + 1]
                )

            inverses[b] = end_pool.tile([P, HEADS], F32, name="inverse")
            nc.scalar.activation(out=inverses[b][:], in_=norm2[b][:], func=ACT.Abs_reciprocal_sqrt)

        def scale_and_store(b, engine, step):
            factor = end_pool.tile([P, HEADS], F32, name="factor")
            nc.vector.tensor_tensor(out=factor[:], in0=inverses[b][:], in1=gains[:], op=MULT)
            result = end_pool.tile([P, HEADS, HEAD_DIM], F32, name="result")
            for h0 in range(0, HEADS, step):
                heads = slice(h0, h0 + step)
                engine.tensor_tensor(
                    out=result[:, heads, :],
                    in0=q_sb[b][:, heads, :],
                    in1=factor[:, heads].unsqueeze(2).to_broadcast([P, step, HEAD_DIM]),
                    op=MULT,
                )
                nc.sync.dma_start(out=out[b, heads].rearrange("h n d -> n h d"), in_=result[:, heads, :])

        def finish_last_batch(unfinished):
            r = len(PIECES) - 1
            for b in unfinished:
                scale_and_store(b, nc.gpsimd, HALF_HEADS)
            add_bias(LAST)
            q = keep.tile([P, HEADS, HEAD_DIM], F32, name="q_last")
            waste = end_pool.tile([P, HEADS, HEAD_DIM], F32, name="waste")
            norm_sum = end_pool.tile([P, HEADS], F32, name="norm2")
            inverse = end_pool.tile([P, HEADS], F32, name="inverse")
            result = end_pool.tile([P, HEADS, HEAD_DIM], F32, name="result")
            factor = end_pool.tile([P, HEADS], F32, name="factor")

            def finish_first_half():
                heads = slice(0, HALF_HEADS)
                nc.vector.tensor_tensor(out=factor[:, heads], in0=inverse[:, heads], in1=gains[:, heads], op=MULT)
                nc.vector.tensor_tensor(
                    out=result[:, heads, :],
                    in0=q[:, heads, :],
                    in1=factor[:, heads].unsqueeze(2).to_broadcast([P, HALF_HEADS, HEAD_DIM]),
                    op=MULT,
                )
                nc.sync.dma_start(out=out[LAST, heads].rearrange("h n d -> n h d"), in_=result[:, heads, :])

            def finish_quarter(quarter):
                h0, h1 = quarter * QUARTER_HEADS, (quarter + 1) * QUARTER_HEADS
                for h in range(h0, h1):
                    nc.vector.scalar_tensor_tensor(
                        out=result[:, h, :],
                        in0=q[:, h, :],
                        scalar=inverse[:, h : h + 1],
                        in1=gains[:, h : h + 1].to_broadcast([P, HEAD_DIM]),
                        op0=MULT,
                        op1=MULT,
                    )
                nc.sync.dma_start(out=out[LAST, h0:h1].rearrange("h n d -> n h d"), in_=result[:, h0:h1, :])

            for quarter in range(QUARTERS):
                quarter_sums = multiply_quarter(r, quarter)
                h0, h1 = quarter * QUARTER_HEADS, (quarter + 1) * QUARTER_HEADS
                nc.vector.tensor_tensor(
                    out=q[:, h0:h1, :],
                    in0=quarter_sums[:],
                    in1=q_sb[LAST][:, h0:h1, :],
                    op=ADD,
                )
                for h in range(h0, h1):
                    nc.scalar.activation(
                        out=waste[:, h, :], in_=q[:, h, :], func=ACT.Square, accum_out=norm_sum[:, h : h + 1]
                    )
                if h1 % HALF_HEADS == 0:
                    half = slice(h1 - HALF_HEADS, h1)
                    nc.scalar.activation(out=inverse[:, half], in_=norm_sum[:, half], func=ACT.Abs_reciprocal_sqrt)
            finish_first_half()
            finish_quarter(2)
            finish_quarter(3)

        pieces = len(PIECES)
        first_full = CHUNK_GROUPS.index(MAX_GROUPS) * BATCHES
        loaded = 0
        cleared = 2

        def load_next():
            c, b = PIECES[loaded]
            load_piece(loaded)
            if loaded == pieces - 1:
                nc.sync.dma_start(out=bias[:].rearrange("p h d -> p (h d)"), in_=bq.partition_broadcast(P))
                nc.sync.dma_start(out=gains[:], in_=gamma.rearrange("a h b c -> (a h b c)").partition_broadcast(P))

        runs = []
        for count in RUN_PIECES:
            start = sum(len(run) for run in runs)
            runs.append(range(start, start + count))
        while loaded < first_full:
            load_next()
            loaded += 1

        done = []
        unfinished = []
        sorted_runs = 0
        for i in range(-2, len(runs)):
            for b in done:
                add_bias(b)
            ahead = min(i + (2 if i < DEEPER else 3), len(runs) - 1)
            while sorted_runs <= ahead:
                for r in runs[sorted_runs]:
                    sort_piece(r)
                sorted_runs += 1
            if 0 <= i + 1 < len(runs):
                for r in runs[i + 1]:
                    flip_piece(r)
                for r in runs[i + 1]:
                    quantise_piece(r)
            for b in done:
                sum_squares(b)
                if i == len(runs) - 2:
                    unfinished.append(b)
                else:
                    scale_and_store(b, nc.vector, HEADS)
            done = []
            if 0 <= i < len(runs) - 1:
                for r in runs[i]:
                    multiply_piece(r)
                    c, b = PIECES[r]
                    if c == CHUNKS - 1 and b != LAST:
                        done.append(b)
            sorted_to = runs[sorted_runs - 1].stop
            for r in range(loaded, min(loaded + 2, pieces, max(first_full, sorted_to) + RAW_BUFS)):
                if PIECES[r] == (cleared, 0):
                    clear_planes(cleared)
                    cleared += 1
                load_next()
                loaded += 1
        finish_last_batch(unfinished)
